import numpy as np
import ml_dtypes


def mxq(x, axis, fmt="e4m3"):
    dtype, down = {"e4m3": (ml_dtypes.float8_e4m3fn, 7), "e5m2": (ml_dtypes.float8_e5m2, 14)}[fmt]
    v = np.moveaxis(np.asarray(x, np.float32).astype(ml_dtypes.bfloat16).astype(np.float64), axis, -1)
    blocks = v.reshape(v.shape[:-1] + (-1, 32))
    amax = np.abs(blocks).max(-1, keepdims=True)
    byte = np.maximum(np.where(amax > 0, np.frexp(amax)[1] - 1 + 127, 0) - down, 1)
    scale = np.exp2(byte - 127.0)
    codes = (blocks / scale).astype(np.float32).astype(dtype).astype(np.float64)
    return np.moveaxis((codes * scale).reshape(v.shape), -1, axis)


WIDE = False


def mx_kscale(k):
    if not WIDE:
        return np.ones(k)
    levels = np.array([10, -10, 5, -5, 0])
    if k % 512:
        return np.exp2(np.random.permutation(np.resize(levels, k // 32))).repeat(32)
    a = np.empty((k // 512, 16))
    for p in range(k // 512):
        a[p, :8] = np.random.permutation(np.resize(levels, 8))
        for g in range(8):
            far = levels[np.abs(levels - a[p, g]) >= 10]
            a[p, g + 8] = far[np.random.randint(len(far))]
    return np.exp2(a.ravel()).repeat(32)


BF16 = ml_dtypes.bfloat16


def bf(x):
    return np.asarray(x, np.float32).astype(BF16)


def f64(x):
    return np.asarray(x).astype(np.float64)


B, D, G, S, K, E, H, C1, C2, C3 = 256, 1024, 16, 256, 256, 2, 1024, 8, 64, 128
EPS = 1e-5


def sigmoid(v):
    return 1.0 / (1.0 + np.exp(-v))


def setup_inputs():
    t = mx_kscale(H)
    return {"le": bf(np.maximum(np.random.standard_normal((B, G, S)), 0.0) * 1.25),
            "ew1": bf(np.random.standard_normal((E, H, S)) * 1.2 / np.sqrt(S)),
            "ew2": bf(np.random.standard_normal((E, K, H)) * 3.0 / np.sqrt(H) / t),
            "ebg": bf((1.0 + 0.1 * np.random.standard_normal((E, G, H))) * t),
            "ebb": bf(0.3 * np.random.standard_normal((E, G, H)) * t),
            "ebm": bf(0.3 * np.random.standard_normal((E, G, H))),
            "ebv": bf(0.5 + np.random.uniform(size=(E, G, H)))}


def reference(le, ew1, ew2, ebg, ebb, ebm, ebv):
    u = (f64(le).reshape(B * G, S) @ f64(ew1).transpose(0, 2, 1)).reshape(E, B, G, H)
    gain = f64(ebg) / np.sqrt(f64(ebv) + EPS)
    h = np.maximum((u - f64(ebm)[:, None]) * gain[:, None] + f64(ebb)[:, None], 0.0)
    hq = mxq(h.reshape(E, B * G, H), 2, "e4m3")
    out = (hq @ mxq(f64(ew2), 2, "e4m3").transpose(0, 2, 1)).reshape(E, B, G, K)
    sel = sigmoid(out[0])
    sel = np.clip(1.2 * sel - 0.1, 0.0, 1.0)
    layer_bias = out[E - 1]
    return sel, layer_bias

@@ -1,0 +1,350 @@
+from contextlib import ExitStack
+
+import concourse.mybir as mybir
+from concourse.masks import make_identity
+
+F32 = mybir.dt.float32
+BF16 = mybir.dt.bfloat16
+U32 = mybir.dt.uint32
+U8 = mybir.dt.uint8
+FP8X4 = mybir.dt.float8_e4m3fn_x4
+ACT = mybir.ActivationFunctionType
+ALU = mybir.AluOpType
+
+P = 128
+B, G, S, H, K, E = 256, 16, 256, 1024, 256, 2
+EPS = 1e-5
+FLOPS = 2 * B * G * S * H * E + 2 * B * G * H * K * E
+
+PIN = False
+SPREAD = True
+FULL = [(rg, e, (0, 1)) for rg in range(8) for e in range(2)]
+GROUPS = FULL[:-1] + [(7, 1, (0,)), (7, 1, (1,))] if False else FULL
+NG = len(GROUPS)
+NU = 2 * NG
+LE_CHUNKS = ((0, 2), (2, 4), (4, 8), (8, 16))
+
+
+def on_vector(n, j):
+    return (n == 0 and j % 2 == 1) or (n > 0 and j == 0 and n % 2 == 1)
+
+
+def copy_engine(hh):
+    return "v"
+
+
+LE_ENG = "s"
+W2_ENG = "v"
+
+
+def tile_tgnetworkbias_pa_t_kernel(tc, le, ew1, ew2, ebg, ebb, ebm, ebv, out_0, out_1):
+    nc = tc.nc
+    with ExitStack() as ctx:
+        const = ctx.enter_context(tc.tile_pool(name="const", bufs=1))
+        hbp = ctx.enter_context(tc.tile_pool(name="hbp", bufs=3))
+        grp = ctx.enter_context(tc.tile_pool(name="grp", bufs=3))
+        cdp = ctx.enter_context(tc.tile_pool(name="cdp", bufs=8))
+        outp = ctx.enter_context(tc.tile_pool(name="outp", bufs=6))
+        ps1 = ctx.enter_context(tc.psum_pool(name="ps1", bufs=6))
+        ps2 = ctx.enter_context(tc.psum_pool(name="ps2", bufs=2))
+
+        if PIN:
+            ctx.enter_context(tc.manual_schedule())
+
+        le_v = le.rearrange("(bh p) g s -> p bh (g s)", p=P)
+        le_raw = {}
+
+        def load_le(q, ci):
+            g0, g1 = LE_CHUNKS[ci]
+            t = const.tile([P, 2 * (g1 - g0) * S], BF16, name="leraw%d" % ci)
+            q.dma_start(out=t[:].rearrange("p (bh x) -> p bh x", bh=2), in_=le_v[:, :, g0 * S:g1 * S])
+            le_raw[ci] = t
+
+        w1raw = {}
+
+        def load_w1(q, e, c):
+            t = const.tile([P, 1024], BF16, name="w1raw%d%d" % (e, c))
+            q.dma_start(out=t[:], in_=ew1[e, c * 512:(c + 1) * 512, :].rearrange("(p t) s -> p (t s)", t=4))
+            w1raw[(e, c)] = t
+
+        w2raw = {}
+
+        def load_w2(q, e):
+            t = const.tile([P, 2048], BF16, name="w2raw%d" % e)
+            q.dma_start(out=t[:].rearrange("p (kb h) -> p kb h", kb=2),
+                        in_=ew2[e].rearrange("(kb p) h -> p kb h", p=P))
+            w2raw[e] = t
+
+        load_le(nc.scalar, 0)
+        load_w1(nc.scalar, 0, 0)
+        load_w1(nc.scalar, 0, 1)
+        bn_raw = []
+        for i, pair in enumerate(((ebv, ebg), (ebm, ebb))):
+            t = const.tile([P, 512], BF16, name="bnraw%d" % i)
+            for k, src in enumerate(pair):
+                nc.sync.dma_start(out=t[k * 64:(k + 1) * 64, :], in_=src.rearrange("e g (c x) -> (e g c) x", x=512))
+            bn_raw.append(t)
+        load_w1(nc.sync, 1, 0)
+        load_w1(nc.sync, 1, 1)
+        load_w2(nc.sync, 0)
+        load_le(nc.sync, 1)
+        load_w2(nc.sync, 1)
+        load_le(nc.sync, 2)
+        load_le(nc.sync, 3)
+
+        ident = const.tile([P, P], F32, name="ident")
+        make_identity(nc, ident[:])
+
+        eps_t = const.tile([P, 1], F32, name="eps_t")
+        nc.vector.memset(eps_t[:], EPS)
+        warm = const.tile([P, 1], F32, name="warm")
+        nc.scalar.activation(out=warm[:], in_=eps_t[:], func=ACT.Abs_reciprocal_sqrt)
+        gain = const.tile([P, 256], F32, name="gain")
+        shift = const.tile([P, 256], F32, name="shift")
+
+        def bn_finish(pt):
+            v = pt[:].bitcast(BF16).rearrange("p (i u k x) -> p i k u x", i=2, u=2, k=2)
+            vv, vg, vm, vb = v[:, 0, 0], v[:, 0, 1], v[:, 1, 0], v[:, 1, 1]
+
+            def cols(t):
+                return t[:].rearrange("p (u x) -> p u x", u=2)
+
+            r = const.tile([P, 256], F32, name="r")
+            nc.scalar.activation(out=cols(r), in_=vv, func=ACT.Abs_reciprocal_sqrt, bias=eps_t[:, 0:1], scale=1.0)
+            hv = const.tile([P, 256], F32, name="hv")
+            nc.vector.tensor_scalar(out=cols(hv), in0=vv, scalar1=EPS, scalar2=-0.5, op0=ALU.add, op1=ALU.mult)
+            w = const.tile([P, 256], F32, name="w")
+            for it in range(2):
+                nc.vector.tensor_tensor(out=w[:], in0=r[:], in1=hv[:], op=ALU.mult)
+                nc.vector.tensor_tensor(out=w[:], in0=w[:], in1=r[:], op=ALU.mult)
+                nc.vector.scalar_tensor_tensor(out=r[:], in0=w[:], scalar=1.5, in1=r[:], op0=ALU.add, op1=ALU.mult)
+            nc.vector.tensor_tensor(out=cols(gain), in0=vg, in1=cols(r), op=ALU.mult)
+            nc.vector.tensor_tensor(out=cols(w), in0=vm, in1=cols(gain), op=ALU.mult)
+            nc.vector.tensor_tensor(out=cols(shift), in0=vb, in1=cols(w), op=ALU.subtract)
+
+        def copy_out(eng, dst, srcv):
+            if eng == "s":
+                nc.scalar.copy(out=dst, in_=srcv)
+            else:
+                nc.vector.tensor_copy(out=dst, in_=srcv)
+
+        jobs = []
+        cursor = {"next": 0}
+
+        def run_one_step():
+            if cursor["next"] < len(jobs):
+                jobs[cursor["next"]]()
+                cursor["next"] = cursor["next"] + 1
+
+        def flush_steps():
+            for k in range(len(jobs) - cursor["next"]):
+                run_one_step()
+
+        def add_job(sources, finish):
+            box = {}
+
+            def step(i):
+                if i == 0:
+                    pt_new = ps1.tile([P, 512], F32, name="u")
+                    box["pt"] = pt_new
+                nc.tensor.transpose(box["pt"][:, i * P:(i + 1) * P], sources[i], ident[:])
+                if i == 3:
+                    finish(box["pt"])
+
+            for i in range(4):
+                jobs.append(lambda i=i: step(i))
+
+        def prm_transposes():
+            add_job([bn_raw[i][:].bitcast(F32)[:, u:256:2] for i in range(2) for u in range(2)], bn_finish)
+
+        leT = {}
+
+        def le_transposes(rg, eng):
+            ci = [i for i, (g0, g1) in enumerate(LE_CHUNKS) if g0 <= 2 * rg < g1][0]
+            g0, g1 = LE_CHUNKS[ci]
+            words = le_raw[ci][:].bitcast(F32)
+            offs = [(bh * (g1 - g0) + 2 * rg + gi - g0) * P for gi in range(2) for bh in range(2)]
+            t = const.tile([P, 512], F32, name="leT%d" % rg)
+            add_job([words[:, o:o + P] for o in offs], lambda pt: copy_out(eng, t[:], pt[:]))
+            leT[rg] = t
+
+        w1T = {}
+
+        def w1_transposes(e, c, eng):
+            words = w1raw[(e, c)][:].bitcast(F32)
+            t = const.tile([P, 512], F32, name="w1T%d%d" % (e, c))
+            add_job([words[:, j * P:(j + 1) * P] for j in range(4)], lambda pt: copy_out(eng, t[:], pt[:]))
+            w1T[(e, c)] = t
+
+        w2c = {}
+        w2s = {}
+
+        def w2_prepare(e, eng):
+            words = w2raw[e][:].bitcast(F32)
+            g2 = const.tile([P, 2048], BF16, name="w2g%d" % e, align_bytes=64)
+            g2w = g2[:].bitcast(F32)
+            cw = const.tile([P, 512], U32, name="w2c%d" % e, align_bytes=64)
+            sw = const.tile([P, 512], U8, name="w2s%d" % e, align_bytes=64)
+
+            def finish(c, pt):
+                copy_out(eng, g2w[:, c * 512:(c + 1) * 512].rearrange("p (k u) -> p k u", u=2),
+                         pt[:].rearrange("p (u k) -> p k u", u=2))
+                if c == 1:
+                    nc.vector.quantize_mx(out=cw[:].bitcast(FP8X4), scales=sw[:], in_=g2[:])
+
+            for c in range(2):
+                add_job([words[:, kb * 512 + c * 256 + u:kb * 512 + (c + 1) * 256:2] for u in range(2) for kb in range(2)],
+                        lambda pt, c=c: finish(c, pt))
+            w2c[e] = cw
+            w2s[e] = sw
+
+        ups = {}
+        hbs = {}
+        grs = {}
+        cds = {}
+        o2s = {}
+        sgs = {}
+
+        def bank_pe(n, j):
+            rg, e, gis = GROUPS[n // 2]
+            c = n % 2
+            wd = 256 * len(gis)
+            u_ps = ps1.tile([P, 512], F32, name="u")
+            wv = w1T[(e, c)][:].bitcast(BF16).rearrange("q (x a) -> q x a", a=2)
+            xv = leT[rg][:].bitcast(BF16).rearrange("q (x a) -> q x a", a=2)
+            for a in range(2):
+                nc.tensor.matmul(u_ps[:, 0:wd], lhsT=wv[:, j * P:(j + 1) * P, a], rhs=xv[:, gis[0] * 256:gis[0] * 256 + wd, a],
+                                 start=(a == 0), stop=(a == 1))
+                if SPREAD:
+                    run_one_step()
+            ups[(n, j)] = u_ps
+
+        def bank_bn(n, j):
+            rg, e, gis = GROUPS[n // 2]
+            c = n % 2
+            wd = 256 * len(gis)
+            if j == 0:
+                hb_new = hbp.tile([P, 2048], BF16, name="hb")
+                hbs[n] = hb_new
+            hb = hbs[n]
+            u_ps = ups[(n, j)]
+            for i, gi in enumerate(gis):
+                cs = (j // 2) * P + ((e * G + 2 * rg + gi) * 2 + c) * 2 + j % 2
+                dst = hb[:, j * wd + i * 256:j * wd + (i + 1) * 256]
+                srcv = u_ps[:, i * 256:(i + 1) * 256]
+                if on_vector(n, j):
+                    nc.vector.tensor_scalar(out=dst, in0=srcv, scalar1=gain[:, cs:cs + 1], scalar2=shift[:, cs:cs + 1],
+                                            op0=ALU.mult, op1=ALU.add)
+                else:
+                    nc.scalar.activation(out=dst, in_=srcv, func=ACT.Relu, bias=shift[:, cs:cs + 1], scale=gain[:, cs:cs + 1])
+
+        def regroup(n):
+            wd = 256 * len(GROUPS[n // 2][2])
+            gr = grp.tile([P, 2048], BF16, name="gr", align_bytes=64)
+            dst = gr[:, 0:4 * wd].rearrange("p (c i t) -> p c t i", i=4, t=4)
+            srcv = hbs[n][:, 0:4 * wd].rearrange("p (t c i) -> p c t i", t=4, i=4)
+            nc.vector.tensor_scalar_max(out=dst, in0=srcv, scalar1=0.0)
+            grs[n] = gr
+
+        def quantise(n):
+            cd = cdp.tile([P, 512], U32, name="cd", align_bytes=64)
+            sc = cdp.tile([P, 512], U8, name="sc", align_bytes=64)
+            wd = 256 * len(GROUPS[n // 2][2])
+            nc.vector.quantize_mx(out=cd[:, 0:wd].bitcast(FP8X4), scales=sc[:, 0:wd], in_=grs[n][:, 0:4 * wd])
+            cds[n] = (cd, sc)
+
+        def stage2(hh):
+            su, bh = hh // 2, hh % 2
+            rg, e, gis = GROUPS[su]
+            o2 = ps2.tile([P, 512], F32, name="o2")
+            for gi in range(len(gis)):
+                for c in range(2):
+                    cd, sc = cds[2 * su + c]
+                    cols = slice(gi * 256 + bh * P, gi * 256 + (bh + 1) * P)
+                    nc.tensor.matmul_mx(
+                        out=o2[:, gi * 256:(gi + 1) * 256],
+                        lhsT=cd[:, cols].bitcast(FP8X4), lhsT_scale=sc[:, cols],
+                        rhs=w2c[e][:, c * 256:(c + 1) * 256].bitcast(FP8X4), rhs_scale=w2s[e][:, c * 256:(c + 1) * 256],
+                        start=(c == 0), stop=(c == 1))
+            o2s[hh] = o2
+
+        out_v = [o.rearrange("(bh p) g k -> p bh (g k)", p=P) for o in (out_0, out_1)]
+
+        def evac_first(hh):
+            sg = outp.tile([P, 512], F32, name="sg")
+            rg, e, gis = GROUPS[hh // 2]
+            wd = 256 * len(gis)
+            if e == 0:
+                nc.scalar.activation(out=sg[:, 0:wd], in_=o2s[hh][:, 0:wd], func=ACT.Sigmoid)
+            else:
+                copy_out(copy_engine(hh), sg[:, 0:wd], o2s[hh][:, 0:wd])
+            sgs[hh] = sg
+
+        def evac_second(hh):
+            sg = sgs[hh]
+            su, bh = hh // 2, hh % 2
+            rg, e, gis = GROUPS[su]
+            wd = 256 * len(gis)
+            if e == 0:
+                nc.vector.tensor_scalar(out=sg[:, 0:wd], in0=sg[:, 0:wd], scalar1=1.2, scalar2=-0.1, op0=ALU.mult, op1=ALU.add)
+                nc.vector.tensor_scalar(out=sg[:, 0:wd], in0=sg[:, 0:wd], scalar1=0.0, scalar2=1.0, op0=ALU.max, op1=ALU.min)
+            o = rg * 512 + gis[0] * 256
+            nc.sync.dma_start(out=out_v[e][:, bh, o:o + wd], in_=sg[:, 0:wd])
+
+        le_transposes(0, "s")
+        w1_transposes(0, 0, "s")
+        flush_steps()
+        prm_transposes()
+        w1_transposes(0, 1, "s")
+        if not SPREAD:
+            bank_pe(0, 0)
+            bank_pe(0, 1)
+            flush_steps()
+            bank_pe(0, 2)
+            bank_pe(0, 3)
+        else:
+            for j in range(4):
+                bank_pe(0, j)
+        nc.scalar.activation(out=warm[:], in_=eps_t[:], func=ACT.Sigmoid)
+        for j in range(4):
+            bank_bn(0, j)
+
+        for n in range(NU + 4):
+            for j in range(4):
+                if SPREAD:
+                    if (n, j) == (1, 0):
+                        w1_transposes(1, 0, "s")
+                        w1_transposes(1, 1, "s")
+                    if (n, j) == (2, 0):
+                        w2_prepare(0, W2_ENG)
+                    if (n, j) == (3, 0):
+                        le_transposes(1, LE_ENG)
+                    if (n, j) == (4, 0):
+                        w2_prepare(1, W2_ENG)
+                    if j == 0 and n % 4 == 1 and 2 <= n // 4 + 1 < 8 and n < 32:
+                        le_transposes(n // 4 + 1, LE_ENG)
+                else:
+                    if (n, j) == (1, 2):
+                        w1_transposes(1, 0, "s")
+                        w1_transposes(1, 1, "s")
+                    if (n, j) == (2, 2):
+                        w2_prepare(0, W2_ENG)
+                    if (n, j) == (4, 2):
+                        w2_prepare(1, W2_ENG)
+                    if j == 0 and n % 4 == 1 and n // 4 + 1 < 8 and n < 32:
+                        le_transposes(n // 4 + 1, LE_ENG)
+                    flush_steps()
+                if 1 <= n < NU:
+                    bank_pe(n, j)
+                    bank_bn(n, j)
+                if j == 0:
+                    if 0 <= n - 4 < NU:
+                        evac_first(n - 4)
+                    if 0 <= n - 1 < NU:
+                        regroup(n - 1)
+                if j == 1 and 0 <= n - 1 < NU:
+                    quantise(n - 1)
+                if j == 2 and 0 <= n - 4 < NU:
+                    evac_second(n - 4)
+                if j == 3 and 0 <= n - 3 < NU:
+                    stage2(n - 3)

@@ -75,15 +75,15 @@ def tile_tgnetworkbias_pa_t_kernel(tc, le, ew1, ew2, ebg, ebb, ebm, ebv, out_0, 
                         in_=ew2[e].rearrange("(kb p) h -> p kb h", p=P))
             w2raw[e] = t
 
-        load_le(nc.scalar, 0)
-        load_w1(nc.scalar, 0, 0)
-        load_w1(nc.scalar, 0, 1)
         bn_raw = []
         for i, pair in enumerate(((ebv, ebg), (ebm, ebb))):
             t = const.tile([P, 512], BF16, name="bnraw%d" % i)
             for k, src in enumerate(pair):
                 nc.sync.dma_start(out=t[k * 64:(k + 1) * 64, :], in_=src.rearrange("e g (c x) -> (e g c) x", x=512))
             bn_raw.append(t)
+        load_le(nc.scalar, 0)
+        load_w1(nc.scalar, 0, 0)
+        load_w1(nc.scalar, 0, 1)
         load_w1(nc.sync, 1, 0)
         load_w1(nc.sync, 1, 1)
         load_w2(nc.sync, 0)
@@ -106,21 +106,32 @@ def tile_tgnetworkbias_pa_t_kernel(tc, le, ew1, ew2, ebg, ebb, ebm, ebv, out_0, 
             v = pt[:].bitcast(BF16).rearrange("p (i u k x) -> p i k u x", i=2, u=2, k=2)
             vv, vg, vm, vb = v[:, 0, 0], v[:, 0, 1], v[:, 1, 0], v[:, 1, 1]
 
-            def cols(t):
-                return t[:].rearrange("p (u x) -> p u x", u=2)
+            def cols(t, e):
+                return t[:].rearrange("p (u e x) -> p u e x", u=2, e=2)[:, :, e]
+
+            def half(x, e):
+                return x.rearrange("p u (e x) -> p u e x", e=2)[:, :, e]
 
             r = const.tile([P, 256], F32, name="r")
-            nc.scalar.activation(out=cols(r), in_=vv, func=ACT.Abs_reciprocal_sqrt, bias=eps_t[:, 0:1], scale=1.0)
             hv = const.tile([P, 256], F32, name="hv")
-            nc.vector.tensor_scalar(out=cols(hv), in0=vv, scalar1=EPS, scalar2=-0.5, op0=ALU.add, op1=ALU.mult)
             w = const.tile([P, 256], F32, name="w")
-            for it in range(2):
-                nc.vector.tensor_tensor(out=w[:], in0=r[:], in1=hv[:], op=ALU.mult)
-                nc.vector.tensor_tensor(out=w[:], in0=w[:], in1=r[:], op=ALU.mult)
-                nc.vector.scalar_tensor_tensor(out=r[:], in0=w[:], scalar=1.5, in1=r[:], op0=ALU.add, op1=ALU.mult)
-            nc.vector.tensor_tensor(out=cols(gain), in0=vg, in1=cols(r), op=ALU.mult)
-            nc.vector.tensor_tensor(out=cols(w), in0=vm, in1=cols(gain), op=ALU.mult)
-            nc.vector.tensor_tensor(out=cols(shift), in0=vb, in1=cols(w), op=ALU.subtract)
+            gr = const.tile([P, 256], F32, name="gr0")
+            for e in range(2):
+                nc.scalar.activation(out=cols(r, e), in_=half(vv, e), func=ACT.Abs_reciprocal_sqrt, bias=eps_t[:, 0:1], scale=1.0)
+            for e in range(2):
+                nc.vector.tensor_scalar(out=cols(hv, e), in0=half(vv, e), scalar1=EPS, scalar2=-0.5, op0=ALU.add, op1=ALU.mult)
+            for e in range(2):
+                nc.vector.tensor_tensor(out=cols(w, e), in0=cols(r, e), in1=cols(hv, e), op=ALU.mult)
+            for e in range(2):
+                nc.vector.tensor_tensor(out=cols(gr, e), in0=half(vg, e), in1=cols(r, e), op=ALU.mult)
+            for e in range(2):
+                nc.vector.tensor_tensor(out=cols(w, e), in0=cols(w, e), in1=cols(r, e), op=ALU.mult)
+            for e in range(2):
+                nc.vector.scalar_tensor_tensor(out=cols(gain, e), in0=cols(w, e), scalar=1.5, in1=cols(gr, e), op0=ALU.add, op1=ALU.mult)
+            for e in range(2):
+                nc.vector.tensor_tensor(out=cols(w, e), in0=half(vm, e), in1=cols(gain, e), op=ALU.mult)
+            for e in range(2):
+                nc.vector.tensor_tensor(out=cols(shift, e), in0=half(vb, e), in1=cols(w, e), op=ALU.subtract)
 
         def copy_out(eng, dst, srcv):
             if eng == "s":
@@ -173,7 +184,12 @@ def tile_tgnetworkbias_pa_t_kernel(tc, le, ew1, ew2, ebg, ebb, ebm, ebv, out_0, 
         def w1_transposes(e, c, eng):
             words = w1raw[(e, c)][:].bitcast(F32)
             t = const.tile([P, 512], F32, name="w1T%d%d" % (e, c))
-            add_job([words[:, j * P:(j + 1) * P] for j in range(4)], lambda pt: copy_out(eng, t[:], pt[:]))
+            def finish(pt):
+                copy_out(eng, t[:], pt[:])
+                if (e, c) == (0, 0):
+                    nc.scalar.activation(out=warm[:], in_=t[:].bitcast(BF16)[:, 0:1], func=ACT.Sigmoid)
+
+            add_job([words[:, j * P:(j + 1) * P] for j in range(4)], finish)
             w1T[(e, c)] = t
 
         w2c = {}
@@ -291,11 +307,11 @@ def tile_tgnetworkbias_pa_t_kernel(tc, le, ew1, ew2, ebg, ebb, ebm, ebv, out_0, 
             o = rg * 512 + gis[0] * 256
             nc.sync.dma_start(out=out_v[e][:, bh, o:o + wd], in_=sg[:, 0:wd])
 
+        prm_transposes()
         le_transposes(0, "s")
         w1_transposes(0, 0, "s")
+        w1_transposes(0, 1, "v")
         flush_steps()
-        prm_transposes()
-        w1_transposes(0, 1, "s")
         if not SPREAD:
             bank_pe(0, 0)
             bank_pe(0, 1)
@@ -305,7 +321,6 @@ def tile_tgnetworkbias_pa_t_kernel(tc, le, ew1, ew2, ebg, ebb, ebm, ebv, out_0, 
         else:
             for j in range(4):
                 bank_pe(0, j)
-        nc.scalar.activation(out=warm[:], in_=eps_t[:], func=ACT.Sigmoid)
         for j in range(4):
             bank_bn(0, j)
 

@@ -16,21 +16,15 @@ B, G, S, H, K, E = 256, 16, 256, 1024, 256, 2
 EPS = 1e-5
 FLOPS = 2 * B * G * S * H * E + 2 * B * G * H * K * E
 
-PIN = False
-SPREAD = True
-FULL = [(rg, e, (0, 1)) for rg in range(8) for e in range(2)]
-GROUPS = FULL[:-1] + [(7, 1, (0,)), (7, 1, (1,))] if False else FULL
+GROUPS = [(rg, e, (0, 1)) for rg in range(6) for e in range(2)] + [(rg, e, (0, 1)) for e in range(2) for rg in (6, 7)]
 NG = len(GROUPS)
 NU = 2 * NG
+LAG = 5
 LE_CHUNKS = ((0, 2), (2, 4), (4, 8), (8, 16))
 
 
 def on_vector(n, j):
-    return (n == 0 and j % 2 == 1) or (n > 0 and j == 0 and n % 2 == 1)
-
-
-def copy_engine(hh):
-    return "v"
+    return n % 4 == 2 and j == 0
 
 
 LE_ENG = "s"
@@ -43,13 +37,12 @@ def tile_tgnetworkbias_pa_t_kernel(tc, le, ew1, ew2, ebg, ebb, ebm, ebv, out_0, 
         const = ctx.enter_context(tc.tile_pool(name="const", bufs=1))
         hbp = ctx.enter_context(tc.tile_pool(name="hbp", bufs=3))
         grp = ctx.enter_context(tc.tile_pool(name="grp", bufs=3))
-        cdp = ctx.enter_context(tc.tile_pool(name="cdp", bufs=8))
-        outp = ctx.enter_context(tc.tile_pool(name="outp", bufs=6))
+        cdp = ctx.enter_context(tc.tile_pool(name="cdp", bufs=12))
+        outp = ctx.enter_context(tc.tile_pool(name="outp", bufs=10))
         ps1 = ctx.enter_context(tc.psum_pool(name="ps1", bufs=6))
         ps2 = ctx.enter_context(tc.psum_pool(name="ps2", bufs=2))
 
-        if PIN:
-            ctx.enter_context(tc.manual_schedule())
+        ctx.enter_context(tc.manual_schedule(engines={mybir.EngineType.PE, mybir.EngineType.Activation, mybir.EngineType.DVE}))
 
         le_v = le.rearrange("(bh p) g s -> p bh (g s)", p=P)
         le_raw = {}
@@ -79,9 +72,9 @@ def tile_tgnetworkbias_pa_t_kernel(tc, le, ew1, ew2, ebg, ebb, ebm, ebv, out_0, 
         for i, pair in enumerate(((ebv, ebg), (ebm, ebb))):
             t = const.tile([P, 512], BF16, name="bnraw%d" % i)
             for k, src in enumerate(pair):
-                nc.sync.dma_start(out=t[k * 64:(k + 1) * 64, :], in_=src.rearrange("e g (c x) -> (e g c) x", x=512))
+                (nc.sync, nc.scalar)[i].dma_start(out=t[k * 64:(k + 1) * 64, :], in_=src.rearrange("e g (c x) -> (e g c) x", x=512))
             bn_raw.append(t)
-        load_le(nc.scalar, 0)
+        load_le(nc.sync, 0)
         load_w1(nc.scalar, 0, 0)
         load_w1(nc.scalar, 0, 1)
         load_w1(nc.sync, 1, 0)
@@ -231,8 +224,7 @@ def tile_tgnetworkbias_pa_t_kernel(tc, le, ew1, ew2, ebg, ebb, ebm, ebv, out_0, 
             for a in range(2):
                 nc.tensor.matmul(u_ps[:, 0:wd], lhsT=wv[:, j * P:(j + 1) * P, a], rhs=xv[:, gis[0] * 256:gis[0] * 256 + wd, a],
                                  start=(a == 0), stop=(a == 1))
-                if SPREAD:
-                    run_one_step()
+                run_one_step()
             ups[(n, j)] = u_ps
 
         def bank_bn(n, j):
@@ -254,112 +246,144 @@ def tile_tgnetworkbias_pa_t_kernel(tc, le, ew1, ew2, ebg, ebb, ebm, ebv, out_0, 
                 else:
                     nc.scalar.activation(out=dst, in_=srcv, func=ACT.Relu, bias=shift[:, cs:cs + 1], scale=gain[:, cs:cs + 1])
 
-        def regroup(n):
-            wd = 256 * len(GROUPS[n // 2][2])
-            gr = grp.tile([P, 2048], BF16, name="gr", align_bytes=64)
-            dst = gr[:, 0:4 * wd].rearrange("p (c i t) -> p c t i", i=4, t=4)
-            srcv = hbs[n][:, 0:4 * wd].rearrange("p (t c i) -> p c t i", t=4, i=4)
+        def regroup(n, t0=0, t1=512):
+            if t0 == 0:
+                gr_new = grp.tile([P, 2048], BF16, name="gr", align_bytes=64)
+                grs[n] = gr_new
+            dst = grs[n][:, 4 * t0:4 * t1].rearrange("p (c i t) -> p c t i", i=4, t=4)
+            srcv = hbs[n][:].rearrange("p (t x) -> p t x", t=4)[:, :, t0:t1].rearrange("p t (c i) -> p c t i", i=4)
             nc.vector.tensor_scalar_max(out=dst, in0=srcv, scalar1=0.0)
-            grs[n] = gr
 
-        def quantise(n):
-            cd = cdp.tile([P, 512], U32, name="cd", align_bytes=64)
-            sc = cdp.tile([P, 512], U8, name="sc", align_bytes=64)
-            wd = 256 * len(GROUPS[n // 2][2])
-            nc.vector.quantize_mx(out=cd[:, 0:wd].bitcast(FP8X4), scales=sc[:, 0:wd], in_=grs[n][:, 0:4 * wd])
-            cds[n] = (cd, sc)
+        def quantise(n, t0=0, t1=512):
+            if t0 == 0:
+                cd_new = cdp.tile([P, 512], U32, name="cd", align_bytes=64)
+                sc_new = cdp.tile([P, 512], U8, name="sc", align_bytes=64)
+                cds[n] = (cd_new, sc_new)
+            cd, sc = cds[n]
+            nc.vector.quantize_mx(out=cd[:, t0:t1].bitcast(FP8X4), scales=sc[:, t0:t1], in_=grs[n][:, 4 * t0:4 * t1])
 
-        def stage2(hh):
-            su, bh = hh // 2, hh % 2
-            rg, e, gis = GROUPS[su]
-            o2 = ps2.tile([P, 512], F32, name="o2")
-            for gi in range(len(gis)):
-                for c in range(2):
-                    cd, sc = cds[2 * su + c]
-                    cols = slice(gi * 256 + bh * P, gi * 256 + (bh + 1) * P)
-                    nc.tensor.matmul_mx(
-                        out=o2[:, gi * 256:(gi + 1) * 256],
-                        lhsT=cd[:, cols].bitcast(FP8X4), lhsT_scale=sc[:, cols],
-                        rhs=w2c[e][:, c * 256:(c + 1) * 256].bitcast(FP8X4), rhs_scale=w2s[e][:, c * 256:(c + 1) * 256],
-                        start=(c == 0), stop=(c == 1))
+        def stage2_open(hh, tail):
+            if tail:
+                o2 = ps1.tile([P, 512], F32, name="u")
+            else:
+                o2 = ps2.tile([P, 512], F32, name="o2")
             o2s[hh] = o2
+
+        def stage2_part(hh, gi):
+            su, bh = hh // 2, hh % 2
+            e = GROUPS[su][1]
+            cols = slice(gi * 256 + bh * P, gi * 256 + (bh + 1) * P)
+            for c in range(2):
+                cd, sc = cds[2 * su + c]
+                nc.tensor.matmul_mx(
+                    out=o2s[hh][:, gi * 256:(gi + 1) * 256],
+                    lhsT=cd[:, cols].bitcast(FP8X4), lhsT_scale=sc[:, cols],
+                    rhs=w2c[e][:, c * 256:(c + 1) * 256].bitcast(FP8X4), rhs_scale=w2s[e][:, c * 256:(c + 1) * 256],
+                    start=(c == 0), stop=(c == 1))
+
+        def stage2(hh, tail=False):
+            stage2_open(hh, tail)
+            for gi in range(2):
+                stage2_part(hh, gi)
 
         out_v = [o.rearrange("(bh p) g k -> p bh (g k)", p=P) for o in (out_0, out_1)]
 
-        def evac_first(hh):
+        def expert(hh):
+            return GROUPS[hh // 2][1]
+
+        def evac(hh, eng="v"):
             sg = outp.tile([P, 512], F32, name="sg")
-            rg, e, gis = GROUPS[hh // 2]
-            wd = 256 * len(gis)
-            if e == 0:
-                nc.scalar.activation(out=sg[:, 0:wd], in_=o2s[hh][:, 0:wd], func=ACT.Sigmoid)
+            if expert(hh) == 0:
+                nc.scalar.activation(out=sg[:], in_=o2s[hh][:], func=ACT.Sigmoid)
             else:
-                copy_out(copy_engine(hh), sg[:, 0:wd], o2s[hh][:, 0:wd])
+                copy_out(eng, sg[:], o2s[hh][:])
             sgs[hh] = sg
 
-        def evac_second(hh):
-            sg = sgs[hh]
-            su, bh = hh // 2, hh % 2
-            rg, e, gis = GROUPS[su]
-            wd = 256 * len(gis)
-            if e == 0:
-                nc.vector.tensor_scalar(out=sg[:, 0:wd], in0=sg[:, 0:wd], scalar1=1.2, scalar2=-0.1, op0=ALU.mult, op1=ALU.add)
-                nc.vector.tensor_scalar(out=sg[:, 0:wd], in0=sg[:, 0:wd], scalar1=0.0, scalar2=1.0, op0=ALU.max, op1=ALU.min)
-            o = rg * 512 + gis[0] * 256
-            nc.sync.dma_start(out=out_v[e][:, bh, o:o + wd], in_=sg[:, 0:wd])
+        def shift_sel(hh):
+            nc.vector.tensor_scalar(out=sgs[hh][:], in0=sgs[hh][:], scalar1=1.2, scalar2=-0.1, op0=ALU.mult, op1=ALU.add)
+
+        def clip_sel(hh):
+            nc.vector.tensor_scalar(out=sgs[hh][:], in0=sgs[hh][:], scalar1=0.0, scalar2=1.0, op0=ALU.max, op1=ALU.min)
+
+        def store(hh, k0=0, k1=512):
+            rg = GROUPS[hh // 2][0]
+            nc.sync.dma_start(out=out_v[expert(hh)][:, hh % 2, rg * 512 + k0:rg * 512 + k1], in_=sgs[hh][:, k0:k1])
 
         prm_transposes()
         le_transposes(0, "s")
         w1_transposes(0, 0, "s")
         w1_transposes(0, 1, "v")
         flush_steps()
-        if not SPREAD:
-            bank_pe(0, 0)
-            bank_pe(0, 1)
-            flush_steps()
-            bank_pe(0, 2)
-            bank_pe(0, 3)
-        else:
-            for j in range(4):
-                bank_pe(0, j)
-        for j in range(4):
-            bank_bn(0, j)
+        def is_expert(hh, e):
+            return 0 <= hh < NU and expert(hh) == e
 
-        for n in range(NU + 4):
+        le_turns = {2 * [g[0] for g in GROUPS].index(rg): rg for rg in range(2, 8)}
+        for n in range(NU):
+            if n == 1:
+                w1_transposes(1, 0, "s")
+                w1_transposes(1, 1, "s")
+            if n == 2:
+                w2_prepare(0, W2_ENG)
+            if n == 3:
+                le_transposes(1, LE_ENG)
+            if n == 4:
+                w2_prepare(1, W2_ENG)
+            if n + 3 in le_turns:
+                le_transposes(le_turns[n + 3], LE_ENG)
+            done = n - LAG - 1
             for j in range(4):
-                if SPREAD:
-                    if (n, j) == (1, 0):
-                        w1_transposes(1, 0, "s")
-                        w1_transposes(1, 1, "s")
-                    if (n, j) == (2, 0):
-                        w2_prepare(0, W2_ENG)
-                    if (n, j) == (3, 0):
-                        le_transposes(1, LE_ENG)
-                    if (n, j) == (4, 0):
-                        w2_prepare(1, W2_ENG)
-                    if j == 0 and n % 4 == 1 and 2 <= n // 4 + 1 < 8 and n < 32:
-                        le_transposes(n // 4 + 1, LE_ENG)
-                else:
-                    if (n, j) == (1, 2):
-                        w1_transposes(1, 0, "s")
-                        w1_transposes(1, 1, "s")
-                    if (n, j) == (2, 2):
-                        w2_prepare(0, W2_ENG)
-                    if (n, j) == (4, 2):
-                        w2_prepare(1, W2_ENG)
-                    if j == 0 and n % 4 == 1 and n // 4 + 1 < 8 and n < 32:
-                        le_transposes(n // 4 + 1, LE_ENG)
-                    flush_steps()
-                if 1 <= n < NU:
-                    bank_pe(n, j)
-                    bank_bn(n, j)
-                if j == 0:
-                    if 0 <= n - 4 < NU:
-                        evac_first(n - 4)
-                    if 0 <= n - 1 < NU:
-                        regroup(n - 1)
-                if j == 1 and 0 <= n - 1 < NU:
-                    quantise(n - 1)
-                if j == 2 and 0 <= n - 4 < NU:
-                    evac_second(n - 4)
-                if j == 3 and 0 <= n - 3 < NU:
-                    stage2(n - 3)
+                bank_pe(n, j)
+                bank_bn(n, j)
+                if j == 1:
+                    if is_expert(done, 0):
+                        evac(done)
+                    if n >= LAG:
+                        stage2(n - LAG)
+            if n >= 1:
+                regroup(n - 1)
+            if is_expert(done, 1):
+                evac(done)
+                store(done)
+            if is_expert(done - 1, 0):
+                clip_sel(done - 1)
+                store(done - 1)
+            if n >= 1:
+                quantise(n - 1)
+            if is_expert(done, 0):
+                shift_sel(done)
+
+        last = NU - 1
+        first = NU - LAG
+        pending = list(range(first, NU - 2))
+        for hh in pending:
+            stage2(hh, True)
+        for gi in range(2):
+            regroup(last, gi * 256, (gi + 1) * 256)
+        if is_expert(first - 2, 0):
+            clip_sel(first - 2)
+            store(first - 2)
+        for gi in range(2):
+            quantise(last, gi * 256, (gi + 1) * 256)
+        for hh in [first - 1] + pending:
+            evac(hh, "s")
+            if expert(hh) == 1:
+                store(hh)
+        sel = [hh for hh in [first - 1] + pending if expert(hh) == 0]
+        stage2_open(NU - 2, True)
+        stage2_open(NU - 1, True)
+        for gi in range(2):
+            for hh in (NU - 2, NU - 1):
+                stage2_part(hh, gi)
+        for hh in sel:
+            shift_sel(hh)
+        for hh in sel:
+            clip_sel(hh)
+            store(hh)
+        for hh in (NU - 2, NU - 1):
+            sg = outp.tile([P, 512], F32, name="sg")
+            sgs[hh] = sg
+        for gi in range(2):
+            cols = slice(gi * 256, (gi + 1) * 256)
+            for hh in (NU - 2, NU - 1):
+                nc.scalar.copy(out=sgs[hh][:, cols], in_=o2s[hh][:, cols])
+                store(hh, gi * 256, (gi + 1) * 256)

@@ -24,7 +24,7 @@ LE_CHUNKS = ((0, 2), (2, 4), (4, 8), (8, 16))
 
 
 def on_vector(n, j):
-    return n % 4 == 2 and j == 0
+    return False
 
 
 LE_ENG = "s"

@@ -224,7 +224,6 @@ def tile_tgnetworkbias_pa_t_kernel(tc, le, ew1, ew2, ebg, ebb, ebm, ebv, out_0, 
             for a in range(2):
                 nc.tensor.matmul(u_ps[:, 0:wd], lhsT=wv[:, j * P:(j + 1) * P, a], rhs=xv[:, gis[0] * 256:gis[0] * 256 + wd, a],
                                  start=(a == 0), stop=(a == 1))
-                run_one_step()
             ups[(n, j)] = u_ps
 
         def bank_bn(n, j):
@@ -334,6 +333,9 @@ def tile_tgnetworkbias_pa_t_kernel(tc, le, ew1, ew2, ebg, ebb, ebm, ebv, out_0, 
             for j in range(4):
                 bank_pe(n, j)
                 bank_bn(n, j)
+                if j % 2 == 0:
+                    for k in range(4):
+                        run_one_step()
                 if j == 1:
                     if is_expert(done, 0):
                         evac(done)

from contextlib import ExitStack

import concourse.mybir as mybir
from concourse.masks import make_identity

F32 = mybir.dt.float32
BF16 = mybir.dt.bfloat16
U32 = mybir.dt.uint32
U8 = mybir.dt.uint8
FP8X4 = mybir.dt.float8_e4m3fn_x4
ACT = mybir.ActivationFunctionType
ALU = mybir.AluOpType

P = 128
B, G, S, H, K, E = 256, 16, 256, 1024, 256, 2
EPS = 1e-5
FLOPS = 2 * B * G * S * H * E + 2 * B * G * H * K * E

GROUPS = [(rg, e, (0, 1)) for rg in range(6) for e in range(2)] + [(rg, e, (0, 1)) for e in range(2) for rg in (6, 7)]
NG = len(GROUPS)
NU = 2 * NG
LAG = 5
LE_CHUNKS = ((0, 2), (2, 4), (4, 8), (8, 16))


def on_vector(n, j):
    return False


LE_ENG = "s"
W2_ENG = "v"


def tile_tgnetworkbias_pa_t_kernel(tc, le, ew1, ew2, ebg, ebb, ebm, ebv, out_0, out_1):
    nc = tc.nc
    with ExitStack() as ctx:
        const = ctx.enter_context(tc.tile_pool(name="const", bufs=1))
        hbp = ctx.enter_context(tc.tile_pool(name="hbp", bufs=3))
        grp = ctx.enter_context(tc.tile_pool(name="grp", bufs=3))
        cdp = ctx.enter_context(tc.tile_pool(name="cdp", bufs=12))
        outp = ctx.enter_context(tc.tile_pool(name="outp", bufs=10))
        ps1 = ctx.enter_context(tc.psum_pool(name="ps1", bufs=6))
        ps2 = ctx.enter_context(tc.psum_pool(name="ps2", bufs=2))

        ctx.enter_context(tc.manual_schedule(engines={mybir.EngineType.PE, mybir.EngineType.Activation, mybir.EngineType.DVE}))

        le_v = le.rearrange("(bh p) g s -> p bh (g s)", p=P)
        le_raw = {}

        def load_le(q, ci):
            g0, g1 = LE_CHUNKS[ci]
            t = const.tile([P, 2 * (g1 - g0) * S], BF16, name="leraw%d" % ci)
            q.dma_start(out=t[:].rearrange("p (bh x) -> p bh x", bh=2), in_=le_v[:, :, g0 * S:g1 * S])
            le_raw[ci] = t

        w1raw = {}

        def load_w1(q, e, c):
            t = const.tile([P, 1024], BF16, name="w1raw%d%d" % (e, c))
            q.dma_start(out=t[:], in_=ew1[e, c * 512:(c + 1) * 512, :].rearrange("(p t) s -> p (t s)", t=4))
            w1raw[(e, c)] = t

        w2raw = {}

        def load_w2(q, e):
            t = const.tile([P, 2048], BF16, name="w2raw%d" % e)
            q.dma_start(out=t[:].rearrange("p (kb h) -> p kb h", kb=2),
                        in_=ew2[e].rearrange("(kb p) h -> p kb h", p=P))
            w2raw[e] = t

        bn_raw = []
        for i, pair in enumerate(((ebv, ebg), (ebm, ebb))):
            t = const.tile([P, 512], BF16, name="bnraw%d" % i)
            for k, src in enumerate(pair):
                (nc.sync, nc.scalar)[i].dma_start(out=t[k * 64:(k + 1) * 64, :], in_=src.rearrange("e g (c x) -> (e g c) x", x=512))
            bn_raw.append(t)
        load_le(nc.sync, 0)
        load_w1(nc.scalar, 0, 0)
        load_w1(nc.scalar, 0, 1)
        load_w1(nc.sync, 1, 0)
        load_w1(nc.sync, 1, 1)
        load_w2(nc.sync, 0)
        load_le(nc.sync, 1)
        load_w2(nc.sync, 1)
        load_le(nc.sync, 2)
        load_le(nc.sync, 3)

        ident = const.tile([P, P], F32, name="ident")
        make_identity(nc, ident[:])

        eps_t = const.tile([P, 1], F32, name="eps_t")
        nc.vector.memset(eps_t[:], EPS)
        warm = const.tile([P, 1], F32, name="warm")
        nc.scalar.activation(out=warm[:], in_=eps_t[:], func=ACT.Abs_reciprocal_sqrt)
        gain = const.tile([P, 256], F32, name="gain")
        shift = const.tile([P, 256], F32, name="shift")

        def bn_finish(pt):
            v = pt[:].bitcast(BF16).rearrange("p (i u k x) -> p i k u x", i=2, u=2, k=2)
            vv, vg, vm, vb = v[:, 0, 0], v[:, 0, 1], v[:, 1, 0], v[:, 1, 1]

            def cols(t, e):
                return t[:].rearrange("p (u e x) -> p u e x", u=2, e=2)[:, :, e]

            def half(x, e):
                return x.rearrange("p u (e x) -> p u e x", e=2)[:, :, e]

            r = const.tile([P, 256], F32, name="r")
            hv = const.tile([P, 256], F32, name="hv")
            w = const.tile([P, 256], F32, name="w")
            gr = const.tile([P, 256], F32, name="gr0")
            for e in range(2):
                nc.scalar.activation(out=cols(r, e), in_=half(vv, e), func=ACT.Abs_reciprocal_sqrt, bias=eps_t[:, 0:1], scale=1.0)
            for e in range(2):
                nc.vector.tensor_scalar(out=cols(hv, e), in0=half(vv, e), scalar1=EPS, scalar2=-0.5, op0=ALU.add, op1=ALU.mult)
            for e in range(2):
                nc.vector.tensor_tensor(out=cols(w, e), in0=cols(r, e), in1=cols(hv, e), op=ALU.mult)
            for e in range(2):
                nc.vector.tensor_tensor(out=cols(gr, e), in0=half(vg, e), in1=cols(r, e), op=ALU.mult)
            for e in range(2):
                nc.vector.tensor_tensor(out=cols(w, e), in0=cols(w, e), in1=cols(r, e), op=ALU.mult)
            for e in range(2):
                nc.vector.scalar_tensor_tensor(out=cols(gain, e), in0=cols(w, e), scalar=1.5, in1=cols(gr, e), op0=ALU.add, op1=ALU.mult)
            for e in range(2):
                nc.vector.tensor_tensor(out=cols(w, e), in0=half(vm, e), in1=cols(gain, e), op=ALU.mult)
            for e in range(2):
                nc.vector.tensor_tensor(out=cols(shift, e), in0=half(vb, e), in1=cols(w, e), op=ALU.subtract)

        def copy_out(eng, dst, srcv):
            if eng == "s":
                nc.scalar.copy(out=dst, in_=srcv)
            else:
                nc.vector.tensor_copy(out=dst, in_=srcv)

        jobs = []
        cursor = {"next": 0}

        def run_one_step():
            if cursor["next"] < len(jobs):
                jobs[cursor["next"]]()
                cursor["next"] = cursor["next"] + 1

        def flush_steps():
            for k in range(len(jobs) - cursor["next"]):
                run_one_step()

        def add_job(sources, finish):
            box = {}

            def step(i):
                if i == 0:
                    pt_new = ps1.tile([P, 512], F32, name="u")
                    box["pt"] = pt_new
                nc.tensor.transpose(box["pt"][:, i * P:(i + 1) * P], sources[i], ident[:])
                if i == 3:
                    finish(box["pt"])

            for i in range(4):
                jobs.append(lambda i=i: step(i))

        def prm_transposes():
            add_job([bn_raw[i][:].bitcast(F32)[:, u:256:2] for i in range(2) for u in range(2)], bn_finish)

        leT = {}

        def le_transposes(rg, eng):
            ci = [i for i, (g0, g1) in enumerate(LE_CHUNKS) if g0 <= 2 * rg < g1][0]
            g0, g1 = LE_CHUNKS[ci]
            words = le_raw[ci][:].bitcast(F32)
            offs = [(bh * (g1 - g0) + 2 * rg + gi - g0) * P for gi in range(2) for bh in range(2)]
            t = const.tile([P, 512], F32, name="leT%d" % rg)
            add_job([words[:, o:o + P] for o in offs], lambda pt: copy_out(eng, t[:], pt[:]))
            leT[rg] = t

        w1T = {}

        def w1_transposes(e, c, eng):
            words = w1raw[(e, c)][:].bitcast(F32)
            t = const.tile([P, 512], F32, name="w1T%d%d" % (e, c))
            def finish(pt):
                copy_out(eng, t[:], pt[:])
                if (e, c) == (0, 0):
                    nc.scalar.activation(out=warm[:], in_=t[:].bitcast(BF16)[:, 0:1], func=ACT.Sigmoid)

            add_job([words[:, j * P:(j + 1) * P] for j in range(4)], finish)
            w1T[(e, c)] = t

        w2c = {}
        w2s = {}

        def w2_prepare(e, eng):
            words = w2raw[e][:].bitcast(F32)
            g2 = const.tile([P, 2048], BF16, name="w2g%d" % e, align_bytes=64)
            g2w = g2[:].bitcast(F32)
            cw = const.tile([P, 512], U32, name="w2c%d" % e, align_bytes=64)
            sw = const.tile([P, 512], U8, name="w2s%d" % e, align_bytes=64)

            def finish(c, pt):
                copy_out(eng, g2w[:, c * 512:(c + 1) * 512].rearrange("p (k u) -> p k u", u=2),
                         pt[:].rearrange("p (u k) -> p k u", u=2))
                if c == 1:
                    nc.vector.quantize_mx(out=cw[:].bitcast(FP8X4), scales=sw[:], in_=g2[:])

            for c in range(2):
                add_job([words[:, kb * 512 + c * 256 + u:kb * 512 + (c + 1) * 256:2] for u in range(2) for kb in range(2)],
                        lambda pt, c=c: finish(c, pt))
            w2c[e] = cw
            w2s[e] = sw

        ups = {}
        hbs = {}
        grs = {}
        cds = {}
        o2s = {}
        sgs = {}

        def bank_pe(n, j):
            rg, e, gis = GROUPS[n // 2]
            c = n % 2
            wd = 256 * len(gis)
            u_ps = ps1.tile([P, 512], F32, name="u")
            wv = w1T[(e, c)][:].bitcast(BF16).rearrange("q (x a) -> q x a", a=2)
            xv = leT[rg][:].bitcast(BF16).rearrange("q (x a) -> q x a", a=2)
            for a in range(2):
                nc.tensor.matmul(u_ps[:, 0:wd], lhsT=wv[:, j * P:(j + 1) * P, a], rhs=xv[:, gis[0] * 256:gis[0] * 256 + wd, a],
                                 start=(a == 0), stop=(a == 1))
            ups[(n, j)] = u_ps

        def bank_bn(n, j):
            rg, e, gis = GROUPS[n // 2]
            c = n % 2
            wd = 256 * len(gis)
            if j == 0:
                hb_new = hbp.tile([P, 2048], BF16, name="hb")
                hbs[n] = hb_new
            hb = hbs[n]
            u_ps = ups[(n, j)]
            for i, gi in enumerate(gis):
                cs = (j // 2) * P + ((e * G + 2 * rg + gi) * 2 + c) * 2 + j % 2
                dst = hb[:, j * wd + i * 256:j * wd + (i + 1) * 256]
                srcv = u_ps[:, i * 256:(i + 1) * 256]
                if on_vector(n, j):
                    nc.vector.tensor_scalar(out=dst, in0=srcv, scalar1=gain[:, cs:cs + 1], scalar2=shift[:, cs:cs + 1],
                                            op0=ALU.mult, op1=ALU.add)
                else:
                    nc.scalar.activation(out=dst, in_=srcv, func=ACT.Relu, bias=shift[:, cs:cs + 1], scale=gain[:, cs:cs + 1])

        def regroup(n, t0=0, t1=512):
            if t0 == 0:
                gr_new = grp.tile([P, 2048], BF16, name="gr", align_bytes=64)
                grs[n] = gr_new
            dst = grs[n][:, 4 * t0:4 * t1].rearrange("p (c i t) -> p c t i", i=4, t=4)
            srcv = hbs[n][:].rearrange("p (t x) -> p t x", t=4)[:, :, t0:t1].rearrange("p t (c i) -> p c t i", i=4)
            nc.vector.tensor_scalar_max(out=dst, in0=srcv, scalar1=0.0)

        def quantise(n, t0=0, t1=512):
            if t0 == 0:
                cd_new = cdp.tile([P, 512], U32, name="cd", align_bytes=64)
                sc_new = cdp.tile([P, 512], U8, name="sc", align_bytes=64)
                cds[n] = (cd_new, sc_new)
            cd, sc = cds[n]
            nc.vector.quantize_mx(out=cd[:, t0:t1].bitcast(FP8X4), scales=sc[:, t0:t1], in_=grs[n][:, 4 * t0:4 * t1])

        def stage2_open(hh, tail):
            if tail:
                o2 = ps1.tile([P, 512], F32, name="u")
            else:
                o2 = ps2.tile([P, 512], F32, name="o2")
            o2s[hh] = o2

        def stage2_part(hh, gi):
            su, bh = hh // 2, hh % 2
            e = GROUPS[su][1]
            cols = slice(gi * 256 + bh * P, gi * 256 + (bh + 1) * P)
            for c in range(2):
                cd, sc = cds[2 * su + c]
                nc.tensor.matmul_mx(
                    out=o2s[hh][:, gi * 256:(gi + 1) * 256],
                    lhsT=cd[:, cols].bitcast(FP8X4), lhsT_scale=sc[:, cols],
                    rhs=w2c[e][:, c * 256:(c + 1) * 256].bitcast(FP8X4), rhs_scale=w2s[e][:, c * 256:(c + 1) * 256],
                    start=(c == 0), stop=(c == 1))

        def stage2(hh, tail=False):
            stage2_open(hh, tail)
            for gi in range(2):
                stage2_part(hh, gi)

        out_v = [o.rearrange("(bh p) g k -> p bh (g k)", p=P) for o in (out_0, out_1)]

        def expert(hh):
            return GROUPS[hh // 2][1]

        def evac(hh, eng="v"):
            sg = outp.tile([P, 512], F32, name="sg")
            if expert(hh) == 0:
                nc.scalar.activation(out=sg[:], in_=o2s[hh][:], func=ACT.Sigmoid)
            else:
                copy_out(eng, sg[:], o2s[hh][:])
            sgs[hh] = sg

        def shift_sel(hh):
            nc.vector.tensor_scalar(out=sgs[hh][:], in0=sgs[hh][:], scalar1=1.2, scalar2=-0.1, op0=ALU.mult, op1=ALU.add)

        def clip_sel(hh):
            nc.vector.tensor_scalar(out=sgs[hh][:], in0=sgs[hh][:], scalar1=0.0, scalar2=1.0, op0=ALU.max, op1=ALU.min)

        def store(hh, k0=0, k1=512):
            rg = GROUPS[hh // 2][0]
            nc.sync.dma_start(out=out_v[expert(hh)][:, hh % 2, rg * 512 + k0:rg * 512 + k1], in_=sgs[hh][:, k0:k1])

        prm_transposes()
        le_transposes(0, "s")
        w1_transposes(0, 0, "s")
        w1_transposes(0, 1, "v")
        flush_steps()
        def is_expert(hh, e):
            return 0 <= hh < NU and expert(hh) == e

        le_turns = {2 * [g[0] for g in GROUPS].index(rg): rg for rg in range(2, 8)}
        for n in range(NU):
            if n == 1:
                w1_transposes(1, 0, "s")
                w1_transposes(1, 1, "s")
            if n == 2:
                w2_prepare(0, W2_ENG)
            if n == 3:
                le_transposes(1, LE_ENG)
            if n == 4:
                w2_prepare(1, W2_ENG)
            if n + 3 in le_turns:
                le_transposes(le_turns[n + 3], LE_ENG)
            done = n - LAG - 1
            for j in range(4):
                bank_pe(n, j)
                bank_bn(n, j)
                if j % 2 == 0:
                    for k in range(4):
                        run_one_step()
                if j == 1:
                    if is_expert(done, 0):
                        evac(done)
                    if n >= LAG:
                        stage2(n - LAG)
            if n >= 1:
                regroup(n - 1)
            if is_expert(done, 1):
                evac(done)
                store(done)
            if is_expert(done - 1, 0):
                clip_sel(done - 1)
                store(done - 1)
            if n >= 1:
                quantise(n - 1)
            if is_expert(done, 0):
                shift_sel(done)

        last = NU - 1
        first = NU - LAG
        pending = list(range(first, NU - 2))
        for hh in pending:
            stage2(hh, True)
        for gi in range(2):
            regroup(last, gi * 256, (gi + 1) * 256)
        if is_expert(first - 2, 0):
            clip_sel(first - 2)
            store(first - 2)
        for gi in range(2):
            quantise(last, gi * 256, (gi + 1) * 256)
        for hh in [first - 1] + pending:
            evac(hh, "s")
            if expert(hh) == 1:
                store(hh)
        sel = [hh for hh in [first - 1] + pending if expert(hh) == 0]
        stage2_open(NU - 2, True)
        stage2_open(NU - 1, True)
        for gi in range(2):
            for hh in (NU - 2, NU - 1):
                stage2_part(hh, gi)
        for hh in sel:
            shift_sel(hh)
        for hh in sel:
            clip_sel(hh)
            store(hh)
        for hh in (NU - 2, NU - 1):
            sg = outp.tile([P, 512], F32, name="sg")
            sgs[hh] = sg
        for gi in range(2):
            cols = slice(gi * 256, (gi + 1) * 256)
            for hh in (NU - 2, NU - 1):
                nc.scalar.copy(out=sgs[hh][:, cols], in_=o2s[hh][:, cols])
                store(hh, gi * 256, (gi + 1) * 256)
